import numpy as np
import ml_dtypes


def mxq(x, axis, fmt="e4m3"):
    dtype, down = {"e4m3": (ml_dtypes.float8_e4m3fn, 7), "e5m2": (ml_dtypes.float8_e5m2, 14)}[fmt]
    v = np.moveaxis(np.asarray(x, np.float32).astype(ml_dtypes.bfloat16).astype(np.float64), axis, -1)
    blocks = v.reshape(v.shape[:-1] + (-1, 32))
    amax = np.abs(blocks).max(-1, keepdims=True)
    byte = np.maximum(np.where(amax > 0, np.frexp(amax)[1] - 1 + 127, 0) - down, 1)
    scale = np.exp2(byte - 127.0)
    codes = (blocks / scale).astype(np.float32).astype(dtype).astype(np.float64)
    return np.moveaxis((codes * scale).reshape(v.shape), -1, axis)


WIDE = False


def mx_kscale(k):
    if not WIDE:
        return np.ones(k)
    levels = np.array([10, -10, 5, -5, 0])
    a = np.random.permutation(np.resize(levels, k // 512 * 4)).reshape(k // 512, 4)
    idx = np.arange(k)
    return np.exp2(a[idx // 512, idx % 128 // 32])


BF16 = ml_dtypes.bfloat16


def bf(x):
    return np.asarray(x, np.float32).astype(BF16)


def f64(x):
    return np.asarray(x).astype(np.float64)


B, T, KA, KT, DIM, NH, HD, E = 2, 256, 128, 128, 512, 8, 64, 8
EPS = 1e-5


def setup_inputs():
    r = np.random.standard_normal
    s = mx_kscale(DIM)
    t = mx_kscale(DIM)
    return {"h_attn": bf(r((B, T, DIM)) * 0.4 * s),
            "x": bf(r((B, T, DIM))),
            "W_o": bf(r((DIM, DIM)) * 2.0 / np.sqrt(DIM) / s[None, :]),
            "b_o": bf(r(DIM) * 0.3 + 0.2),
            "W_ffn": bf(r((DIM, DIM)) / np.sqrt(DIM) / t[None, :]),
            "b_ffn": bf(r(DIM) * 0.3),
            "gamma": bf((1.0 + 0.1 * r(DIM)) * t),
            "beta": bf(0.2 * r(DIM) * t)}


def reference(h_attn, x, W_o, b_o, W_ffn, b_ffn, gamma, beta):
    y = (mxq(f64(h_attn), 2, "e4m3") @ mxq(f64(W_o), 1, "e4m3").T) + f64(b_o) + f64(x)
    mu = y.mean(-1, keepdims=True)
    var = ((y - mu) ** 2).mean(-1, keepdims=True)
    xn = (y - mu) / np.sqrt(var + EPS) * f64(gamma) + f64(beta)
    return np.maximum((mxq(xn, 2, "e4m3") @ mxq(f64(W_ffn), 1, "e4m3").T) + f64(b_ffn), 0.0)

@@ -1,0 +1,206 @@
+from contextlib import ExitStack
+
+import concourse.mybir as mybir
+from concourse.masks import make_identity
+
+F32 = mybir.dt.float32
+BF16 = mybir.dt.bfloat16
+U32 = mybir.dt.uint32
+U8 = mybir.dt.uint8
+FP8X4 = mybir.dt.float8_e4m3fn_x4
+ALU = mybir.AluOpType
+ACT = mybir.ActivationFunctionType
+
+P = 128
+DIM = 512
+ROWS = 512
+ROW_TILES = ROWS // P
+PACK = 4
+HALVES = 2
+BANK_TILES = 2
+EPS = 1e-5
+
+FLOPS = 2 * 2 * ROWS * DIM * DIM
+
+
+def transpose_row_tile(nc, part, rows, ident_f32):
+    words = rows.bitcast(F32)
+    for u in range(HALVES):
+        nc.tensor.transpose(part[:, u, :], words[:, u * P : (u + 1) * P], ident_f32[:])
+
+
+def tile_l1regressionmoeactionhead_pc_s_kernel(
+    tc, h_attn, x, W_o, b_o, W_ffn, b_ffn, gamma, beta, out
+):
+    nc = tc.nc
+    with ExitStack() as ctx:
+        keep = ctx.enter_context(tc.tile_pool(name="keep", bufs=1))
+        psum = ctx.enter_context(tc.psum_pool(name="psum", bufs=8))
+
+        h_view = h_attn.flatten_outer_dims().rearrange("(p j) k -> p j k", j=ROW_TILES)
+        x_view = x.flatten_outer_dims().rearrange("(p j) o -> p j o", j=ROW_TILES)
+        out_view = out.flatten_outer_dims().rearrange("(p j) f -> p j f", j=ROW_TILES)
+        wo_view = W_o.rearrange("(j p) k -> p j k", p=P)
+        wf_view = W_ffn.rearrange("(j p) k -> p j k", p=P)
+
+        def load_in_halves(name, view):
+            sb = keep.tile([P, ROW_TILES, DIM], BF16, name=name)
+            for b in range(ROW_TILES // BANK_TILES):
+                tiles = slice(b * BANK_TILES, (b + 1) * BANK_TILES)
+                nc.sync.dma_start(out=sb[:, tiles, :], in_=view[:, tiles, :])
+            return sb
+
+        vec_rows = keep.tile([P, P], BF16)
+        nc.gpsimd.memset(vec_rows[:], 0.0)
+        for v, vec in enumerate((b_o, gamma, beta, b_ffn)):
+            nc.sync.dma_start(
+                out=vec_rows[4 * v : 4 * v + 4, :], in_=vec.rearrange("(t c) -> t c", c=P)
+            )
+        wo_sb = load_in_halves("wo_sb", wo_view)
+        h_sb = load_in_halves("h_sb", h_view)
+        x_sb = keep.tile([P, ROW_TILES, DIM], BF16)
+        nc.sync.dma_start(out=x_sb[:], in_=x_view)
+        wf_sb = load_in_halves("wf_sb", wf_view)
+
+        ident_bf16 = keep.tile([P, P], BF16)
+        make_identity(nc, ident_bf16[:])
+        ident_f32 = keep.tile([P, P], F32)
+        make_identity(nc, ident_f32[:])
+        eps = keep.tile([P, 1], F32)
+        nc.vector.memset(eps[:], EPS)
+        warm = keep.tile([P, 1], F32)
+        nc.scalar.activation(out=warm[:], in_=eps[:], func=ACT.Sqrt)
+
+        def mx_tiles(name):
+            grouped = keep.tile([P, ROWS, PACK], BF16, align_bytes=64, name=name + "_grouped")
+            codes = keep.tile([P, ROWS], U32, align_bytes=64, name=name + "_codes")
+            scales = keep.tile([P, ROWS], U8, align_bytes=64, name=name + "_scales")
+            return grouped, codes, scales
+
+        def regroup_matrix(sb, grouped):
+            for b in range(ROW_TILES // BANK_TILES):
+                bank = psum.tile([P, BANK_TILES, HALVES, P], F32, tag="bank")
+                for i in range(BANK_TILES):
+                    transpose_row_tile(nc, bank[:, i, :, :], sb[:, b * BANK_TILES + i, :], ident_f32)
+                cols = slice(b * BANK_TILES * P, (b + 1) * BANK_TILES * P)
+                nc.scalar.copy(
+                    out=grouped[:].bitcast(F32)[:, cols, :].rearrange(
+                        "p (i r) u -> p i r u", i=BANK_TILES
+                    ),
+                    in_=bank[:].rearrange("p i u r -> p i r u"),
+                )
+
+        def quantise(operand, cols):
+            grouped, codes, scales = operand
+            nc.vector.quantize_mx(
+                out=codes[:, cols].bitcast(FP8X4),
+                scales=scales[:, cols],
+                in_=grouped[:, cols, :].rearrange("p r t -> p (r t)"),
+            )
+
+        def quantise_matrix(operand):
+            for b in range(ROW_TILES // BANK_TILES):
+                quantise(operand, slice(b * BANK_TILES * P, (b + 1) * BANK_TILES * P))
+
+        def multiply(acc, tokens_operand, toks, weights_operand):
+            nc.tensor.matmul_mx(
+                out=acc[:],
+                lhsT=tokens_operand[1][:, toks].bitcast(FP8X4),
+                lhsT_scale=tokens_operand[2][:, toks],
+                rhs=weights_operand[1][:].bitcast(FP8X4),
+                rhs_scale=weights_operand[2][:],
+                start=True,
+                stop=True,
+            )
+
+        vec_bank = psum.tile([P, P], BF16, tag="bank")
+        nc.tensor.transpose(vec_bank[:], vec_rows[:], ident_bf16[:])
+        vec_cols = keep.tile([P, 4 * ROW_TILES], BF16)
+        nc.vector.tensor_copy(out=vec_cols[:], in_=vec_bank[:, 0 : 4 * ROW_TILES])
+
+        def spread(name, v):
+            bank = psum.tile([P, ROW_TILES, P], BF16, tag="bank")
+            for t in range(ROW_TILES):
+                col = 4 * v + t
+                nc.tensor.transpose(
+                    bank[:, t, :], vec_cols[:, col : col + 1].to_broadcast([P, P]), ident_bf16[:]
+                )
+            everywhere = keep.tile([P, DIM], BF16, name=name)
+            nc.scalar.copy(out=everywhere[:], in_=bank[:].rearrange("p t c -> p (t c)"))
+            return everywhere
+
+        wo_mx = mx_tiles("wo")
+        h_mx = mx_tiles("h")
+        wf_mx = mx_tiles("wf")
+        xn_mx = mx_tiles("xn")
+
+        b_o_all = spread("b_o_all", 0)
+        regroup_matrix(wo_sb, wo_mx[0])
+        quantise_matrix(wo_mx)
+        regroup_matrix(h_sb, h_mx[0])
+        quantise_matrix(h_mx)
+
+        xb = keep.tile([P, ROW_TILES, DIM], F32)
+        y = keep.tile([P, ROW_TILES, DIM], F32)
+        y_sum = keep.tile([P, ROW_TILES], F32)
+        squares = keep.tile([P, ROW_TILES, DIM], BF16)
+        sq_sum = keep.tile([P, ROW_TILES], F32)
+        for j in range(ROW_TILES):
+            y_acc = psum.tile([P, DIM], F32, tag="bank")
+            multiply(y_acc, h_mx, slice(j * P, (j + 1) * P), wo_mx)
+            nc.vector.tensor_tensor(out=xb[:, j, :], in0=x_sb[:, j, :], in1=b_o_all[:], op=ALU.add)
+            nc.vector.scalar_tensor_tensor(
+                out=y[:, j, :], in0=y_acc[:], scalar=0.0, in1=xb[:, j, :],
+                op0=ALU.add, op1=ALU.add, accum_out=y_sum[:, j : j + 1],
+            )
+            nc.scalar.activation(
+                out=squares[:, j, :], in_=y[:, j, :], func=ACT.Square,
+                bias=y_sum[:, j : j + 1], scale=-1.0 * DIM, accum_out=sq_sum[:, j : j + 1],
+            )
+        neg_mean = keep.tile([P, ROW_TILES], F32)
+        nc.vector.tensor_scalar_mul(out=neg_mean[:], in0=y_sum[:], scalar1=-1.0 / DIM)
+        std = keep.tile([P, ROW_TILES], F32)
+        nc.scalar.activation(
+            out=std[:], in_=sq_sum[:], func=ACT.Sqrt, bias=eps[:], scale=1.0 / (DIM * DIM * DIM)
+        )
+        rstd = keep.tile([P, ROW_TILES], F32)
+        nc.vector.reciprocal(rstd[:], std[:])
+
+        gamma_all = spread("gamma_all", 1)
+        beta_all = spread("beta_all", 2)
+        regroup_matrix(wf_sb, wf_mx[0])
+        b_ffn_all = spread("b_ffn_all", 3)
+
+        gained = keep.tile([P, ROW_TILES, DIM], F32)
+        for j in range(ROW_TILES):
+            nc.vector.scalar_tensor_tensor(
+                out=gained[:, j, :], in0=y[:, j, :], scalar=neg_mean[:, j : j + 1], in1=gamma_all[:],
+                op0=ALU.add, op1=ALU.mult,
+            )
+        xn = keep.tile([P, ROW_TILES, DIM], BF16)
+        for j in range(ROW_TILES):
+            nc.vector.scalar_tensor_tensor(
+                out=xn[:, j, :], in0=gained[:, j, :], scalar=rstd[:, j : j + 1], in1=beta_all[:],
+                op0=ALU.mult, op1=ALU.add,
+            )
+            xn_bank = psum.tile([P, HALVES, P], F32, tag="bank")
+            transpose_row_tile(nc, xn_bank[:], xn[:, j, :], ident_f32)
+            nc.scalar.copy(
+                out=xn_mx[0][:].bitcast(F32)[:, j * P : (j + 1) * P, :],
+                in_=xn_bank[:].rearrange("p u r -> p r u"),
+            )
+
+        quantise_matrix(wf_mx)
+        o_accs = []
+        for j in range(ROW_TILES):
+            toks = slice(j * P, (j + 1) * P)
+            quantise(xn_mx, toks)
+            o_acc = psum.tile([P, DIM], F32, tag="bank")
+            multiply(o_acc, xn_mx, toks, wf_mx)
+            o_accs.append(o_acc)
+        biased = keep.tile([P, ROW_TILES, DIM], F32)
+        result = keep.tile([P, ROW_TILES, DIM], F32)
+        for j in range(ROW_TILES):
+            nc.vector.tensor_tensor(out=biased[:, j, :], in0=o_accs[j][:], in1=b_ffn_all[:], op=ALU.add)
+            nc.scalar.activation(out=result[:, j, :], in_=biased[:, j, :], func=ACT.Relu)
+            nc.sync.dma_start(out=out_view[:, j, :], in_=result[:, j, :])

@@ -16,17 +16,12 @@ DIM = 512
 ROWS = 512
 ROW_TILES = ROWS // P
 PACK = 4
-HALVES = 2
-BANK_TILES = 2
+WORD_RUNS = 2
+HALF_TILES = 2
+HALF_ROWS = HALF_TILES * P
 EPS = 1e-5
 
 FLOPS = 2 * 2 * ROWS * DIM * DIM
-
-
-def transpose_row_tile(nc, part, rows, ident_f32):
-    words = rows.bitcast(F32)
-    for u in range(HALVES):
-        nc.tensor.transpose(part[:, u, :], words[:, u * P : (u + 1) * P], ident_f32[:])
 
 
 def tile_l1regressionmoeactionhead_pc_s_kernel(
@@ -36,6 +31,7 @@ def tile_l1regressionmoeactionhead_pc_s_kernel(
     with ExitStack() as ctx:
         keep = ctx.enter_context(tc.tile_pool(name="keep", bufs=1))
         psum = ctx.enter_context(tc.psum_pool(name="psum", bufs=8))
+        ctx.enter_context(tc.manual_schedule())
 
         h_view = h_attn.flatten_outer_dims().rearrange("(p j) k -> p j k", j=ROW_TILES)
         x_view = x.flatten_outer_dims().rearrange("(p j) o -> p j o", j=ROW_TILES)
@@ -43,27 +39,29 @@ def tile_l1regressionmoeactionhead_pc_s_kernel(
         wo_view = W_o.rearrange("(j p) k -> p j k", p=P)
         wf_view = W_ffn.rearrange("(j p) k -> p j k", p=P)
 
-        def load_in_halves(name, view):
-            sb = keep.tile([P, ROW_TILES, DIM], BF16, name=name)
-            for b in range(ROW_TILES // BANK_TILES):
-                tiles = slice(b * BANK_TILES, (b + 1) * BANK_TILES)
-                nc.sync.dma_start(out=sb[:, tiles, :], in_=view[:, tiles, :])
-            return sb
+        def load_half(sb, view, half):
+            tiles = slice(half * HALF_TILES, (half + 1) * HALF_TILES)
+            nc.sync.dma_start(out=sb[:, tiles, :], in_=view[:, tiles, :])
 
-        vec_rows = keep.tile([P, P], BF16)
+        vec_rows = keep.tile([P, DIM // WORD_RUNS], BF16)
         nc.gpsimd.memset(vec_rows[:], 0.0)
         for v, vec in enumerate((b_o, gamma, beta, b_ffn)):
-            nc.sync.dma_start(
-                out=vec_rows[4 * v : 4 * v + 4, :], in_=vec.rearrange("(t c) -> t c", c=P)
+            nc.scalar.dma_start(
+                out=vec_rows[WORD_RUNS * v : WORD_RUNS * (v + 1), :],
+                in_=vec.rearrange("(u c) -> u c", u=WORD_RUNS),
             )
-        wo_sb = load_in_halves("wo_sb", wo_view)
-        h_sb = load_in_halves("h_sb", h_view)
+        wo_sb = keep.tile([P, ROW_TILES, DIM], BF16)
+        h_sb = keep.tile([P, ROW_TILES, DIM], BF16)
         x_sb = keep.tile([P, ROW_TILES, DIM], BF16)
+        wf_sb = keep.tile([P, ROW_TILES, DIM], BF16)
         nc.sync.dma_start(out=x_sb[:], in_=x_view)
-        wf_sb = load_in_halves("wf_sb", wf_view)
+        load_half(wo_sb, wo_view, 0)
+        load_half(wo_sb, wo_view, 1)
+        load_half(h_sb, h_view, 0)
+        load_half(h_sb, h_view, 1)
+        load_half(wf_sb, wf_view, 0)
+        load_half(wf_sb, wf_view, 1)
 
-        ident_bf16 = keep.tile([P, P], BF16)
-        make_identity(nc, ident_bf16[:])
         ident_f32 = keep.tile([P, P], F32)
         make_identity(nc, ident_f32[:])
         eps = keep.tile([P, 1], F32)
@@ -77,32 +75,36 @@ def tile_l1regressionmoeactionhead_pc_s_kernel(
             scales = keep.tile([P, ROWS], U8, align_bytes=64, name=name + "_scales")
             return grouped, codes, scales
 
-        def regroup_matrix(sb, grouped):
-            for b in range(ROW_TILES // BANK_TILES):
-                bank = psum.tile([P, BANK_TILES, HALVES, P], F32, tag="bank")
-                for i in range(BANK_TILES):
-                    transpose_row_tile(nc, bank[:, i, :, :], sb[:, b * BANK_TILES + i, :], ident_f32)
-                cols = slice(b * BANK_TILES * P, (b + 1) * BANK_TILES * P)
-                nc.scalar.copy(
-                    out=grouped[:].bitcast(F32)[:, cols, :].rearrange(
-                        "p (i r) u -> p i r u", i=BANK_TILES
-                    ),
-                    in_=bank[:].rearrange("p i u r -> p i r u"),
-                )
+        def regroup(operand, first_col, row_tiles):
+            n = len(row_tiles)
+            bank = psum.tile([P, n, WORD_RUNS, P], F32, tag="bank")
+            for i, rows in enumerate(row_tiles):
+                words = rows.bitcast(F32)
+                for u in range(WORD_RUNS):
+                    nc.tensor.transpose(bank[:, i, u, :], words[:, u * P : (u + 1) * P], ident_f32[:])
+            nc.scalar.copy(
+                out=operand[0][:].bitcast(F32)[:, first_col : first_col + n * P, :].rearrange(
+                    "p (i r) u -> p i r u", i=n
+                ),
+                in_=bank[:].rearrange("p i u r -> p i r u"),
+            )
 
-        def quantise(operand, cols):
+        def regroup_half(operand, sb, half):
+            first = half * HALF_TILES
+            regroup(operand, first * P, [sb[:, first + i, :] for i in range(HALF_TILES)])
+
+        def quantise(operand, first_col, n_cols):
             grouped, codes, scales = operand
+            cols = slice(first_col, first_col + n_cols)
             nc.vector.quantize_mx(
                 out=codes[:, cols].bitcast(FP8X4),
                 scales=scales[:, cols],
                 in_=grouped[:, cols, :].rearrange("p r t -> p (r t)"),
             )
 
-        def quantise_matrix(operand):
-            for b in range(ROW_TILES // BANK_TILES):
-                quantise(operand, slice(b * BANK_TILES * P, (b + 1) * BANK_TILES * P))
-
-        def multiply(acc, tokens_operand, toks, weights_operand):
+        def multiply(tokens_operand, j, weights_operand):
+            toks = slice(j * P, (j + 1) * P)
+            acc = psum.tile([P, DIM], F32, tag="bank")
             nc.tensor.matmul_mx(
                 out=acc[:],
                 lhsT=tokens_operand[1][:, toks].bitcast(FP8X4),
@@ -112,43 +114,43 @@ def tile_l1regressionmoeactionhead_pc_s_kernel(
                 start=True,
                 stop=True,
             )
+            return acc
 
-        vec_bank = psum.tile([P, P], BF16, tag="bank")
-        nc.tensor.transpose(vec_bank[:], vec_rows[:], ident_bf16[:])
-        vec_cols = keep.tile([P, 4 * ROW_TILES], BF16)
-        nc.vector.tensor_copy(out=vec_cols[:], in_=vec_bank[:, 0 : 4 * ROW_TILES])
+        vec_bank = psum.tile([P, P], F32, tag="bank")
+        nc.tensor.transpose(vec_bank[:], vec_rows[:].bitcast(F32), ident_f32[:])
+        vec_cols = keep.tile([P, 4 * WORD_RUNS], F32)
+        nc.vector.tensor_copy(out=vec_cols[:], in_=vec_bank[:, 0 : 4 * WORD_RUNS])
+        spread_all = keep.tile([P, 4, DIM], BF16)
 
-        def spread(name, v):
-            bank = psum.tile([P, ROW_TILES, P], BF16, tag="bank")
-            for t in range(ROW_TILES):
-                col = 4 * v + t
+        def spread(first, n):
+            bank = psum.tile([P, n * WORD_RUNS, P], F32, tag="bank")
+            for i in range(n * WORD_RUNS):
+                col = first * WORD_RUNS + i
                 nc.tensor.transpose(
-                    bank[:, t, :], vec_cols[:, col : col + 1].to_broadcast([P, P]), ident_bf16[:]
+                    bank[:, i, :], vec_cols[:, col : col + 1].to_broadcast([P, P]), ident_f32[:]
                 )
-            everywhere = keep.tile([P, DIM], BF16, name=name)
-            nc.scalar.copy(out=everywhere[:], in_=bank[:].rearrange("p t c -> p (t c)"))
-            return everywhere
+            nc.scalar.copy(
+                out=spread_all[:, first : first + n, :].bitcast(F32).rearrange("p v w -> p (v w)"),
+                in_=bank[:].rearrange("p i c -> p (i c)"),
+            )
+
+        gamma_all = spread_all[:, 1, :]
+        beta_all = spread_all[:, 2, :]
+        b_ffn_all = spread_all[:, 3, :]
 
         wo_mx = mx_tiles("wo")
         h_mx = mx_tiles("h")
         wf_mx = mx_tiles("wf")
         xn_mx = mx_tiles("xn")
 
-        b_o_all = spread("b_o_all", 0)
-        regroup_matrix(wo_sb, wo_mx[0])
-        quantise_matrix(wo_mx)
-        regroup_matrix(h_sb, h_mx[0])
-        quantise_matrix(h_mx)
-
         xb = keep.tile([P, ROW_TILES, DIM], F32)
         y = keep.tile([P, ROW_TILES, DIM], F32)
         y_sum = keep.tile([P, ROW_TILES], F32)
         squares = keep.tile([P, ROW_TILES, DIM], BF16)
         sq_sum = keep.tile([P, ROW_TILES], F32)
-        for j in range(ROW_TILES):
-            y_acc = psum.tile([P, DIM], F32, tag="bank")
-            multiply(y_acc, h_mx, slice(j * P, (j + 1) * P), wo_mx)
-            nc.vector.tensor_tensor(out=xb[:, j, :], in0=x_sb[:, j, :], in1=b_o_all[:], op=ALU.add)
+
+        def residual_and_sums(j):
+            y_acc = multiply(h_mx, j, wo_mx)
             nc.vector.scalar_tensor_tensor(
                 out=y[:, j, :], in0=y_acc[:], scalar=0.0, in1=xb[:, j, :],
                 op0=ALU.add, op1=ALU.add, accum_out=y_sum[:, j : j + 1],
@@ -157,6 +159,20 @@ def tile_l1regressionmoeactionhead_pc_s_kernel(
                 out=squares[:, j, :], in_=y[:, j, :], func=ACT.Square,
                 bias=y_sum[:, j : j + 1], scale=-1.0 * DIM, accum_out=sq_sum[:, j : j + 1],
             )
+
+        spread(0, 1)
+        nc.vector.tensor_tensor(
+            out=xb[:], in0=x_sb[:], in1=spread_all[:, 0:1, :].to_broadcast([P, ROW_TILES, DIM]), op=ALU.add
+        )
+        for operand, sb in ((wo_mx, wo_sb), (h_mx, h_sb)):
+            for half in range(2):
+                regroup_half(operand, sb, half)
+            for half in range(2):
+                quantise(operand, half * HALF_ROWS, HALF_ROWS)
+        spread(1, 2)
+        for j in range(ROW_TILES):
+            residual_and_sums(j)
+
         neg_mean = keep.tile([P, ROW_TILES], F32)
         nc.vector.tensor_scalar_mul(out=neg_mean[:], in0=y_sum[:], scalar1=-1.0 / DIM)
         std = keep.tile([P, ROW_TILES], F32)
@@ -164,43 +180,36 @@ def tile_l1regressionmoeactionhead_pc_s_kernel(
             out=std[:], in_=sq_sum[:], func=ACT.Sqrt, bias=eps[:], scale=1.0 / (DIM * DIM * DIM)
         )
         rstd = keep.tile([P, ROW_TILES], F32)
-        nc.vector.reciprocal(rstd[:], std[:])
 
-        gamma_all = spread("gamma_all", 1)
-        beta_all = spread("beta_all", 2)
-        regroup_matrix(wf_sb, wf_mx[0])
-        b_ffn_all = spread("b_ffn_all", 3)
+        for half in range(2):
+            regroup_half(wf_mx, wf_sb, half)
+        spread(3, 1)
 
         gained = keep.tile([P, ROW_TILES, DIM], F32)
         for j in range(ROW_TILES):
             nc.vector.scalar_tensor_tensor(
-                out=gained[:, j, :], in0=y[:, j, :], scalar=neg_mean[:, j : j + 1], in1=gamma_all[:],
+                out=gained[:, j, :], in0=y[:, j, :], scalar=neg_mean[:, j : j + 1], in1=gamma_all,
                 op0=ALU.add, op1=ALU.mult,
             )
+        nc.vector.reciprocal(rstd[:], std[:])
         xn = keep.tile([P, ROW_TILES, DIM], BF16)
         for j in range(ROW_TILES):
             nc.vector.scalar_tensor_tensor(
-                out=xn[:, j, :], in0=gained[:, j, :], scalar=rstd[:, j : j + 1], in1=beta_all[:],
+                out=xn[:, j, :], in0=gained[:, j, :], scalar=rstd[:, j : j + 1], in1=beta_all,
                 op0=ALU.mult, op1=ALU.add,
             )
-            xn_bank = psum.tile([P, HALVES, P], F32, tag="bank")
-            transpose_row_tile(nc, xn_bank[:], xn[:, j, :], ident_f32)
-            nc.scalar.copy(
-                out=xn_mx[0][:].bitcast(F32)[:, j * P : (j + 1) * P, :],
-                in_=xn_bank[:].rearrange("p u r -> p r u"),
-            )
+        for half in range(2):
+            regroup_half(xn_mx, xn, half)
 
-        quantise_matrix(wf_mx)
-        o_accs = []
-        for j in range(ROW_TILES):
-            toks = slice(j * P, (j + 1) * P)
-            quantise(xn_mx, toks)
-            o_acc = psum.tile([P, DIM], F32, tag="bank")
-            multiply(o_acc, xn_mx, toks, wf_mx)
-            o_accs.append(o_acc)
+        quantise(wf_mx, 0, ROWS)
         biased = keep.tile([P, ROW_TILES, DIM], F32)
         result = keep.tile([P, ROW_TILES, DIM], F32)
+        o_accs = []
+        for half in range(2):
+            quantise(xn_mx, half * HALF_ROWS, HALF_ROWS)
+            for j in range(half * HALF_TILES, (half + 1) * HALF_TILES):
+                o_accs.append(multiply(xn_mx, j, wf_mx))
         for j in range(ROW_TILES):
-            nc.vector.tensor_tensor(out=biased[:, j, :], in0=o_accs[j][:], in1=b_ffn_all[:], op=ALU.add)
+            nc.vector.tensor_tensor(out=biased[:, j, :], in0=o_accs[j][:], in1=b_ffn_all, op=ALU.add)
             nc.scalar.activation(out=result[:, j, :], in_=biased[:, j, :], func=ACT.Relu)
             nc.sync.dma_start(out=out_view[:, j, :], in_=result[:, j, :])

@@ -46,7 +46,7 @@ def tile_l1regressionmoeactionhead_pc_s_kernel(
         vec_rows = keep.tile([P, DIM // WORD_RUNS], BF16)
         nc.gpsimd.memset(vec_rows[:], 0.0)
         for v, vec in enumerate((b_o, gamma, beta, b_ffn)):
-            nc.scalar.dma_start(
+            nc.sync.dma_start(
                 out=vec_rows[WORD_RUNS * v : WORD_RUNS * (v + 1), :],
                 in_=vec.rearrange("(u c) -> u c", u=WORD_RUNS),
             )
@@ -164,12 +164,14 @@ def tile_l1regressionmoeactionhead_pc_s_kernel(
         nc.vector.tensor_tensor(
             out=xb[:], in0=x_sb[:], in1=spread_all[:, 0:1, :].to_broadcast([P, ROW_TILES, DIM]), op=ALU.add
         )
-        for operand, sb in ((wo_mx, wo_sb), (h_mx, h_sb)):
-            for half in range(2):
-                regroup_half(operand, sb, half)
-            for half in range(2):
-                quantise(operand, half * HALF_ROWS, HALF_ROWS)
         spread(1, 2)
+        for half in range(2):
+            regroup_half(wo_mx, wo_sb, half)
+        for half in range(2):
+            quantise(wo_mx, half * HALF_ROWS, HALF_ROWS)
+        for j in range(ROW_TILES):
+            regroup(h_mx, j * P, [h_sb[:, j, :]])
+            quantise(h_mx, j * P, P)
         for j in range(ROW_TILES):
             residual_and_sums(j)
 
@@ -198,17 +200,15 @@ def tile_l1regressionmoeactionhead_pc_s_kernel(
                 out=xn[:, j, :], in0=gained[:, j, :], scalar=rstd[:, j : j + 1], in1=beta_all,
                 op0=ALU.mult, op1=ALU.add,
             )
-        for half in range(2):
-            regroup_half(xn_mx, xn, half)
+            regroup(xn_mx, j * P, [xn[:, j, :]])
 
         quantise(wf_mx, 0, ROWS)
         biased = keep.tile([P, ROW_TILES, DIM], F32)
         result = keep.tile([P, ROW_TILES, DIM], F32)
         o_accs = []
-        for half in range(2):
-            quantise(xn_mx, half * HALF_ROWS, HALF_ROWS)
-            for j in range(half * HALF_TILES, (half + 1) * HALF_TILES):
-                o_accs.append(multiply(xn_mx, j, wf_mx))
+        for j in range(ROW_TILES):
+            quantise(xn_mx, j * P, P)
+            o_accs.append(multiply(xn_mx, j, wf_mx))
         for j in range(ROW_TILES):
             nc.vector.tensor_tensor(out=biased[:, j, :], in0=o_accs[j][:], in1=b_ffn_all, op=ALU.add)
             nc.scalar.activation(out=result[:, j, :], in_=biased[:, j, :], func=ACT.Relu)

from contextlib import ExitStack

import concourse.mybir as mybir
from concourse.masks import make_identity

F32 = mybir.dt.float32
BF16 = mybir.dt.bfloat16
U32 = mybir.dt.uint32
U8 = mybir.dt.uint8
FP8X4 = mybir.dt.float8_e4m3fn_x4
ALU = mybir.AluOpType
ACT = mybir.ActivationFunctionType

P = 128
DIM = 512
ROWS = 512
ROW_TILES = ROWS // P
PACK = 4
WORD_RUNS = 2
HALF_TILES = 2
HALF_ROWS = HALF_TILES * P
EPS = 1e-5

FLOPS = 2 * 2 * ROWS * DIM * DIM


def tile_l1regressionmoeactionhead_pc_s_kernel(
    tc, h_attn, x, W_o, b_o, W_ffn, b_ffn, gamma, beta, out
):
    nc = tc.nc
    with ExitStack() as ctx:
        keep = ctx.enter_context(tc.tile_pool(name="keep", bufs=1))
        psum = ctx.enter_context(tc.psum_pool(name="psum", bufs=8))
        ctx.enter_context(tc.manual_schedule())

        h_view = h_attn.flatten_outer_dims().rearrange("(p j) k -> p j k", j=ROW_TILES)
        x_view = x.flatten_outer_dims().rearrange("(p j) o -> p j o", j=ROW_TILES)
        out_view = out.flatten_outer_dims().rearrange("(p j) f -> p j f", j=ROW_TILES)
        wo_view = W_o.rearrange("(j p) k -> p j k", p=P)
        wf_view = W_ffn.rearrange("(j p) k -> p j k", p=P)

        def load_half(sb, view, half):
            tiles = slice(half * HALF_TILES, (half + 1) * HALF_TILES)
            nc.sync.dma_start(out=sb[:, tiles, :], in_=view[:, tiles, :])

        vec_rows = keep.tile([P, DIM // WORD_RUNS], BF16)
        nc.gpsimd.memset(vec_rows[:], 0.0)
        for v, vec in enumerate((b_o, gamma, beta, b_ffn)):
            nc.sync.dma_start(
                out=vec_rows[WORD_RUNS * v : WORD_RUNS * (v + 1), :],
                in_=vec.rearrange("(u c) -> u c", u=WORD_RUNS),
            )
        wo_sb = keep.tile([P, ROW_TILES, DIM], BF16)
        h_sb = keep.tile([P, ROW_TILES, DIM], BF16)
        x_sb = keep.tile([P, ROW_TILES, DIM], BF16)
        wf_sb = keep.tile([P, ROW_TILES, DIM], BF16)
        nc.sync.dma_start(out=x_sb[:], in_=x_view)
        load_half(wo_sb, wo_view, 0)
        load_half(wo_sb, wo_view, 1)
        load_half(h_sb, h_view, 0)
        load_half(h_sb, h_view, 1)
        load_half(wf_sb, wf_view, 0)
        load_half(wf_sb, wf_view, 1)

        ident_f32 = keep.tile([P, P], F32)
        make_identity(nc, ident_f32[:])
        eps = keep.tile([P, 1], F32)
        nc.vector.memset(eps[:], EPS)
        warm = keep.tile([P, 1], F32)
        nc.scalar.activation(out=warm[:], in_=eps[:], func=ACT.Sqrt)

        def mx_tiles(name):
            grouped = keep.tile([P, ROWS, PACK], BF16, align_bytes=64, name=name + "_grouped")
            codes = keep.tile([P, ROWS], U32, align_bytes=64, name=name + "_codes")
            scales = keep.tile([P, ROWS], U8, align_bytes=64, name=name + "_scales")
            return grouped, codes, scales

        def regroup(operand, first_col, row_tiles):
            n = len(row_tiles)
            bank = psum.tile([P, n, WORD_RUNS, P], F32, tag="bank")
            for i, rows in enumerate(row_tiles):
                words = rows.bitcast(F32)
                for u in range(WORD_RUNS):
                    nc.tensor.transpose(bank[:, i, u, :], words[:, u * P : (u + 1) * P], ident_f32[:])
            nc.scalar.copy(
                out=operand[0][:].bitcast(F32)[:, first_col : first_col + n * P, :].rearrange(
                    "p (i r) u -> p i r u", i=n
                ),
                in_=bank[:].rearrange("p i u r -> p i r u"),
            )

        def regroup_half(operand, sb, half):
            first = half * HALF_TILES
            regroup(operand, first * P, [sb[:, first + i, :] for i in range(HALF_TILES)])

        def quantise(operand, first_col, n_cols):
            grouped, codes, scales = operand
            cols = slice(first_col, first_col + n_cols)
            nc.vector.quantize_mx(
                out=codes[:, cols].bitcast(FP8X4),
                scales=scales[:, cols],
                in_=grouped[:, cols, :].rearrange("p r t -> p (r t)"),
            )

        def multiply(tokens_operand, j, weights_operand):
            toks = slice(j * P, (j + 1) * P)
            acc = psum.tile([P, DIM], F32, tag="bank")
            nc.tensor.matmul_mx(
                out=acc[:],
                lhsT=tokens_operand[1][:, toks].bitcast(FP8X4),
                lhsT_scale=tokens_operand[2][:, toks],
                rhs=weights_operand[1][:].bitcast(FP8X4),
                rhs_scale=weights_operand[2][:],
                start=True,
                stop=True,
            )
            return acc

        vec_bank = psum.tile([P, P], F32, tag="bank")
        nc.tensor.transpose(vec_bank[:], vec_rows[:].bitcast(F32), ident_f32[:])
        vec_cols = keep.tile([P, 4 * WORD_RUNS], F32)
        nc.vector.tensor_copy(out=vec_cols[:], in_=vec_bank[:, 0 : 4 * WORD_RUNS])
        spread_all = keep.tile([P, 4, DIM], BF16)

        def spread(first, n):
            bank = psum.tile([P, n * WORD_RUNS, P], F32, tag="bank")
            for i in range(n * WORD_RUNS):
                col = first * WORD_RUNS + i
                nc.tensor.transpose(
                    bank[:, i, :], vec_cols[:, col : col + 1].to_broadcast([P, P]), ident_f32[:]
                )
            nc.scalar.copy(
                out=spread_all[:, first : first + n, :].bitcast(F32).rearrange("p v w -> p (v w)"),
                in_=bank[:].rearrange("p i c -> p (i c)"),
            )

        gamma_all = spread_all[:, 1, :]
        beta_all = spread_all[:, 2, :]
        b_ffn_all = spread_all[:, 3, :]

        wo_mx = mx_tiles("wo")
        h_mx = mx_tiles("h")
        wf_mx = mx_tiles("wf")
        xn_mx = mx_tiles("xn")

        xb = keep.tile([P, ROW_TILES, DIM], F32)
        y = keep.tile([P, ROW_TILES, DIM], F32)
        y_sum = keep.tile([P, ROW_TILES], F32)
        squares = keep.tile([P, ROW_TILES, DIM], BF16)
        sq_sum = keep.tile([P, ROW_TILES], F32)

        def residual_and_sums(j):
            y_acc = multiply(h_mx, j, wo_mx)
            nc.vector.scalar_tensor_tensor(
                out=y[:, j, :], in0=y_acc[:], scalar=0.0, in1=xb[:, j, :],
                op0=ALU.add, op1=ALU.add, accum_out=y_sum[:, j : j + 1],
            )
            nc.scalar.activation(
                out=squares[:, j, :], in_=y[:, j, :], func=ACT.Square,
                bias=y_sum[:, j : j + 1], scale=-1.0 * DIM, accum_out=sq_sum[:, j : j + 1],
            )

        spread(0, 1)
        nc.vector.tensor_tensor(
            out=xb[:], in0=x_sb[:], in1=spread_all[:, 0:1, :].to_broadcast([P, ROW_TILES, DIM]), op=ALU.add
        )
        spread(1, 2)
        for half in range(2):
            regroup_half(wo_mx, wo_sb, half)
        for half in range(2):
            quantise(wo_mx, half * HALF_ROWS, HALF_ROWS)
        for j in range(ROW_TILES):
            regroup(h_mx, j * P, [h_sb[:, j, :]])
            quantise(h_mx, j * P, P)
        for j in range(ROW_TILES):
            residual_and_sums(j)

        neg_mean = keep.tile([P, ROW_TILES], F32)
        nc.vector.tensor_scalar_mul(out=neg_mean[:], in0=y_sum[:], scalar1=-1.0 / DIM)
        std = keep.tile([P, ROW_TILES], F32)
        nc.scalar.activation(
            out=std[:], in_=sq_sum[:], func=ACT.Sqrt, bias=eps[:], scale=1.0 / (DIM * DIM * DIM)
        )
        rstd = keep.tile([P, ROW_TILES], F32)

        for half in range(2):
            regroup_half(wf_mx, wf_sb, half)
        spread(3, 1)

        gained = keep.tile([P, ROW_TILES, DIM], F32)
        for j in range(ROW_TILES):
            nc.vector.scalar_tensor_tensor(
                out=gained[:, j, :], in0=y[:, j, :], scalar=neg_mean[:, j : j + 1], in1=gamma_all,
                op0=ALU.add, op1=ALU.mult,
            )
        nc.vector.reciprocal(rstd[:], std[:])
        xn = keep.tile([P, ROW_TILES, DIM], BF16)
        for j in range(ROW_TILES):
            nc.vector.scalar_tensor_tensor(
                out=xn[:, j, :], in0=gained[:, j, :], scalar=rstd[:, j : j + 1], in1=beta_all,
                op0=ALU.mult, op1=ALU.add,
            )
            regroup(xn_mx, j * P, [xn[:, j, :]])

        quantise(wf_mx, 0, ROWS)
        biased = keep.tile([P, ROW_TILES, DIM], F32)
        result = keep.tile([P, ROW_TILES, DIM], F32)
        o_accs = []
        for j in range(ROW_TILES):
            quantise(xn_mx, j * P, P)
            o_accs.append(multiply(xn_mx, j, wf_mx))
        for j in range(ROW_TILES):
            nc.vector.tensor_tensor(out=biased[:, j, :], in0=o_accs[j][:], in1=b_ffn_all, op=ALU.add)
            nc.scalar.activation(out=result[:, j, :], in_=biased[:, j, :], func=ACT.Relu)
            nc.sync.dma_start(out=out_view[:, j, :], in_=result[:, j, :])
